import numpy as np
import ml_dtypes


BF16 = ml_dtypes.bfloat16


def bf(x):
    return np.asarray(x, np.float32).astype(BF16)


def f64(x):
    return np.asarray(x).astype(np.float64)


E2M1 = np.array([0.0, 0.5, 1.0, 1.5, 2.0, 3.0, 4.0, 6.0, -0.0, -0.5, -1.0, -1.5, -2.0, -3.0, -4.0, -6.0])


def pack_weight(w, fmt):
    k, n = w.shape
    w = f64(bf(w)).reshape(k // 32, 32, n)
    amax = np.abs(w).max(1)
    if fmt == "e4m3":
        byte = np.frexp(amax)[1] - 1 + 127 - 7
    else:
        mant, ex = np.frexp(amax / 6.0)
        byte = np.where(mant > 0.5, ex, ex - 1) + 127
    byte = np.clip(np.where(amax > 0, byte, 1), 1, 254)
    scaled = (w * np.exp2(127.0 - byte)[:, None, :]).reshape(k, n).astype(np.float32)
    by_word = np.ascontiguousarray(scaled.reshape(k // 512, 128, 4, n).transpose(0, 1, 3, 2))
    if fmt == "e4m3":
        words = by_word.astype(ml_dtypes.float8_e4m3fn).view(np.uint8)
    else:
        c = by_word.astype(ml_dtypes.float4_e2m1fn).view(np.uint8) & 0xF
        words = c[..., 0::2] | (c[..., 1::2] << 4)
    return np.ascontiguousarray(words), np.ascontiguousarray(byte.astype(np.uint8).reshape(k // 512, 16, n))


def unpack_weight(words, scales, fmt):
    g, p, n, _ = words.shape
    if fmt == "e4m3":
        vals = np.ascontiguousarray(words).view(ml_dtypes.float8_e4m3fn).astype(np.float64)
    else:
        nib = np.empty((g, p, n, 4), np.uint8)
        nib[..., 0::2] = words & 0xF
        nib[..., 1::2] = words >> 4
        vals = E2M1[nib]
    vals = vals * np.repeat(np.exp2(scales.astype(np.float64) - 127.0), 8, axis=1)[..., None]
    return vals.transpose(0, 1, 3, 2).reshape(g * 512, n)

def pack4(w):
    words, scales = pack_weight(w, "e2m1")
    return words.reshape(words.shape[0], 128, -1), scales


def unpack4(words, scales):
    return unpack_weight(words.reshape(words.shape[0], 128, -1, 2), scales, "e2m1")


def kspread(k):
    return np.exp2(np.repeat(np.random.randint(-6, 7, k // 32), 32).astype(np.float64))


B, S, D = 128, 2, 2048


def sigmoid(v):
    return 1.0 / (1.0 + np.exp(-v))


def setup_inputs():
    s, t = kspread(D), kspread(D)
    inputs = np.random.standard_normal((B, D)) * s
    inputs_words, inputs_scales = pack4(np.ascontiguousarray(inputs.T))
    h_state = (np.random.standard_normal((B, S, D)) * 0.5 * t).reshape(B, S * D)
    h_state_words, h_state_scales = pack4(np.ascontiguousarray(h_state.reshape(B * S, D).T))
    c_state = bf(np.random.standard_normal((B, S * D)) * 0.5)
    c_upd = bf(np.random.standard_normal((B, S, D)))
    kernel_words, kernel_scales = pack4(np.random.standard_normal((D, 3 * D)) / np.sqrt(D) / s[:, None])
    recurrent_kernel_words, recurrent_kernel_scales = pack4(np.random.standard_normal((D, 3 * D)) / np.sqrt(D) / t[:, None])
    bias = bf(np.random.standard_normal(3 * D) * 0.3)
    return {
        "inputs_words": inputs_words,
        "inputs_scales": inputs_scales,
        "h_state_words": h_state_words,
        "h_state_scales": h_state_scales,
        "c_state": c_state,
        "c_upd": c_upd,
        "kernel_words": kernel_words,
        "kernel_scales": kernel_scales,
        "recurrent_kernel_words": recurrent_kernel_words,
        "recurrent_kernel_scales": recurrent_kernel_scales,
        "bias": bias,
    }


def reference(inputs_words, inputs_scales, h_state_words, h_state_scales, c_state, c_upd, kernel_words, kernel_scales, recurrent_kernel_words, recurrent_kernel_scales, bias):
    h_tm1 = unpack4(h_state_words, h_state_scales).T.reshape(B, S, D)
    c_tm1 = f64(c_state).reshape(B, S, D)
    xz = unpack4(inputs_words, inputs_scales).T @ unpack4(kernel_words, kernel_scales)
    hz = h_tm1 @ unpack4(recurrent_kernel_words, recurrent_kernel_scales)
    z = xz[:, None, :] + hz + f64(bias)
    i = sigmoid(z[..., :D])
    f = sigmoid(z[..., D:2 * D])
    o = sigmoid(z[..., 2 * D:])
    c_new = f * c_tm1 + i * np.tanh(f64(c_upd))
    h_new = o * np.tanh(c_new)
    return h_new.reshape(B, -1), c_new.reshape(B, -1)

@@ -1,0 +1,269 @@
+import concourse.mybir as mybir
+from concourse.masks import make_identity
+
+F32 = mybir.dt.float32
+BF16 = mybir.dt.bfloat16
+I32 = mybir.dt.int32
+U8 = mybir.dt.uint8
+FP4X4 = mybir.dt.float4_e2m1fn_x4
+ACT = mybir.ActivationFunctionType
+ALU = mybir.AluOpType
+
+P = 128
+B, S, D = 128, 2, 2048
+G = D // 512
+N = 512
+NB = D // N
+
+FLOPS = 2 * (B + B * S) * D * 3 * D
+
+
+def tile_rlstmcell_pb_kernel(
+    tc, x_words, x_scales, h_words, h_scales, c_state, c_upd, k_words, k_scales, r_words, r_scales, bias, h_out, c_out
+):
+    nc = tc.nc
+    c_upd = c_upd.rearrange("b s d -> b (s d)")
+
+    with (
+        tc.tile_pool(name="keep", bufs=1) as keep,
+        tc.tile_pool(name="work", bufs=1) as work,
+        tc.psum_pool(name="psum", bufs=8) as psum,
+    ):
+        def u8_tile(name, shape):
+            return keep.tile(shape, U8, name=name, align_bytes=64)
+
+        x_codes = u8_tile("x_codes", [P, G, 2 * B])
+        x_planes = u8_tile("x_planes", [P, G, B])
+        h_raw = u8_tile("h_raw", [P, G, 2 * S * B])
+        h_raw_planes = u8_tile("h_raw_planes", [P, G, S * B])
+        h_codes = u8_tile("h_codes", [P, S, G, 2 * B])
+        h_planes = u8_tile("h_planes", [P, S, G, B])
+        w_codes = {(m, a): u8_tile(f"{m}_codes_{a}", [P, G, 2 * D]) for m in "kr" for a in range(3)}
+        w_planes = {(m, a): u8_tile(f"{m}_planes_{a}", [P, G, D]) for m in "kr" for a in range(2)}
+        for m in "kr":
+            w_planes[m, 2] = w_planes[m, 0]
+        w_src = {"k": (k_words, k_scales), "r": (r_words, r_scales)}
+
+        ident = keep.tile([P, P], BF16, name="ident")
+        bias_rows = keep.tile([P, N], BF16, name="bias_rows")
+        bias_sb = keep.tile([P, 3 * D], BF16, name="bias_sb")
+        cu_sb = keep.tile([P, S * D], BF16, name="cu_sb")
+        c_sb = keep.tile([P, S * D], BF16, name="c_sb")
+        u_sb = keep.tile([P, S * D], F32, name="u_sb")
+        warm = keep.tile([P, 1], F32, name="warm")
+
+        def load_scales(planes, src, passes, cols):
+            for r in range(4):
+                nc.sync.dma_start(
+                    out=planes[r:P:32, passes, :].bitcast(I32),
+                    in_=src[passes, r:16:4, cols].rearrange("g q n -> q g n").bitcast(I32),
+                )
+
+        def load_codes(m, a, p0, p1):
+            nc.sync.dma_start(
+                out=w_codes[m, a][:, p0:p1, :].bitcast(I32),
+                in_=w_src[m][0][p0:p1, :, 2 * D * a : 2 * D * (a + 1)].rearrange("g p n -> p g n").bitcast(I32),
+            )
+
+        def load_w_scales(m, a, p0, p1):
+            load_scales(w_planes[m, a], w_src[m][1], slice(p0, p1), slice(D * a, D * (a + 1)))
+
+        def zero(engine, ap):
+            engine.memset(ap.bitcast(I32), 0)
+
+        def new_acc():
+            acc = psum.tile([P, N], F32, name="acc")
+            return acc
+
+        def mm(acc_ap, lhs, lhs_scale, m, a, g, c0, n):
+            nc.tensor.matmul_mx(
+                out=acc_ap,
+                lhsT=lhs.bitcast(FP4X4),
+                lhsT_scale=lhs_scale,
+                rhs=w_codes[m, a][:, g, 2 * c0 : 2 * (c0 + n)].bitcast(FP4X4),
+                rhs_scale=w_planes[m, a][:, g, c0 : c0 + n],
+                start=(g == 0),
+                stop=(g == G - 1),
+            )
+
+        def x_pass(acc, a, b, g):
+            mm(acc[:], x_codes[:, g, :], x_planes[:, g, :], "k", a, g, N * b, N)
+
+        def h_pass(acc, s, a, g, c0, n):
+            mm(acc[:, 0:n], h_codes[:, s, g, :], h_planes[:, s, g, :], "r", a, g, c0, n)
+
+        def bias_spread(j):
+            acc = new_acc()
+            nc.tensor.matmul(acc[:], lhsT=ident[:, j : j + 1].to_broadcast([P, P]), rhs=bias_rows[:], start=True, stop=True)
+            nc.scalar.copy(out=bias_sb[:, N * j : N * (j + 1)], in_=acc[:])
+
+        def x_drain(acc, a, b):
+            xzb = work.tile([P, N], F32, name="xzb", bufs=6)
+            c0 = D * a + N * b
+            nc.vector.tensor_tensor(out=xzb[:], in0=acc[:], in1=bias_sb[:, c0 : c0 + N], op=ALU.add)
+            return xzb
+
+        def gate(acc, xzb, off, n):
+            z = work.tile([P, N], F32, name="z", bufs=8)
+            nc.vector.tensor_tensor(out=z[:, 0:n], in0=acc[:, 0:n], in1=xzb[:, off : off + n], op=ALU.add)
+            nc.scalar.activation(out=z[:, 0:n], in_=z[:, 0:n], func=ACT.Sigmoid)
+            return z
+
+        def state_cols(s, b):
+            return slice(D * s + N * b, D * s + N * (b + 1))
+
+        with tc.manual_schedule():
+            nc.vector.memset(warm[:], 0.0)
+            zero(nc.vector, x_planes[:])
+            zero(nc.vector, w_planes["k", 0][:, 0, :])
+            nc.vector.memset(bias_rows[:], 0.0)
+            zero(nc.vector, w_planes["k", 0][:, 1:G, :])
+            zero(nc.vector, h_raw_planes[:])
+            nc.scalar.activation(out=warm[:], in_=warm[:], func=ACT.Sigmoid)
+            make_identity(nc, ident[:])
+            nc.gpsimd.dma_start(out=bias_rows[0:12, :], in_=bias.rearrange("(j n) -> j n", n=N))
+            for m, a in (("r", 0), ("k", 1), ("r", 1)):
+                zero(nc.gpsimd, w_planes[m, a][:])
+
+            nc.sync.dma_start(out=x_codes[:].bitcast(I32), in_=x_words.rearrange("g p n -> p g n").bitcast(I32))
+            load_codes("k", 0, 0, 1)
+            load_scales(x_planes, x_scales, slice(0, G), slice(0, B))
+            load_w_scales("k", 0, 0, 1)
+            load_codes("k", 0, 1, 2)
+            nc.sync.dma_start(out=h_raw[:].bitcast(I32), in_=h_words.rearrange("g p n -> p g n").bitcast(I32))
+            load_w_scales("k", 0, 1, G)
+            load_codes("k", 0, 2, 3)
+            load_codes("k", 0, 3, 4)
+            load_scales(h_raw_planes, h_scales, slice(0, G), slice(0, S * B))
+            load_codes("r", 0, 0, 1)
+            load_w_scales("r", 0, 0, G)
+            load_codes("r", 0, 1, 2)
+            load_codes("r", 0, 2, 3)
+            load_codes("r", 0, 3, 4)
+            for s in range(S):
+                nc.sync.dma_start(out=cu_sb[:, D * s : D * (s + 1)], in_=c_upd[:, D * s : D * (s + 1)])
+            def load_gate(a):
+                for m in "kr":
+                    load_codes(m, a, 0, 2)
+                    load_w_scales(m, a, 0, G)
+                    load_codes(m, a, 2, 4)
+
+            load_gate(1)
+            for s in range(S):
+                nc.sync.dma_start(out=c_sb[:, D * s : D * (s + 1)], in_=c_state[:, D * s : D * (s + 1)])
+
+            for j in range(NB):
+                bias_spread(j)
+
+            for s in range(S):
+                nc.vector.tensor_copy(
+                    out=h_codes[:, s, :, :].rearrange("p g (b t) -> p g b t", t=2),
+                    in_=h_raw[:].rearrange("p g (b s t) -> p g b s t", s=S, t=2)[:, :, :, s, :],
+                )
+            for s in range(S):
+                nc.vector.tensor_copy(
+                    out=h_planes[:, s, :, :],
+                    in_=h_raw_planes[:].rearrange("p g (b s) -> p g b s", s=S)[:, :, :, s],
+                )
+
+            def u_chunk(s, half):
+                cols = slice(D * s + D // 2 * half, D * s + D // 2 * (half + 1))
+                nc.scalar.activation(out=u_sb[:, cols], in_=cu_sb[:, cols], func=ACT.Tanh)
+
+            def in_product(s, b, z):
+                cols = state_cols(s, b)
+                nc.gpsimd.tensor_tensor(out=u_sb[:, cols], in0=z[:], in1=u_sb[:, cols], op=ALU.mult)
+
+            def forget_product(s, b, z):
+                nc.gpsimd.tensor_tensor(out=z[:], in0=z[:], in1=c_sb[:, state_cols(s, b)], op=ALU.mult)
+
+            accs = [new_acc() for b in range(NB)]
+            for g in range(G):
+                for b in range(NB):
+                    x_pass(accs[b], 0, b, g)
+            xzbs = [x_drain(accs[b], 0, b) for b in range(NB)]
+            for j in range(NB, 3 * NB):
+                bias_spread(j)
+            z_in = {}
+            for half in range(2):
+                units = [(b, s) for b in (2 * half, 2 * half + 1) for s in range(S)]
+                accs = {unit: new_acc() for unit in units}
+                for g in range(G):
+                    for b, s in units:
+                        h_pass(accs[b, s], s, 0, g, N * b, N)
+                for b, s in units:
+                    z_in[b, s] = gate(accs[b, s], xzbs[b], 0, N)
+                for s in range(S):
+                    u_chunk(s, half)
+                for b, s in units:
+                    in_product(s, b, z_in[b, s])
+
+            load_gate(2)
+
+            def x_gate(a):
+                out = []
+                for b in range(NB):
+                    acc = new_acc()
+                    for g in range(G):
+                        x_pass(acc, a, b, g)
+                    out.append(x_drain(acc, a, b))
+                return out
+
+            h_tiles = {}
+
+            def new_state(b, z_forget):
+                for s in range(S):
+                    cols = state_cols(s, b)
+                    nc.vector.tensor_tensor(out=u_sb[:, cols], in0=z_forget[s][:], in1=u_sb[:, cols], op=ALU.add)
+                for s in range(S):
+                    if b % 2 == 0:
+                        ht = work.tile([P, 2 * N], F32, name="ht", bufs=4)
+                        h_tiles[b // 2, s] = ht
+                    nc.scalar.activation(
+                        out=h_tiles[b // 2, s][:, N * (b % 2) : N * (b % 2 + 1)], in_=u_sb[:, state_cols(s, b)], func=ACT.Tanh
+                    )
+                    if b % 2 == 1:
+                        cols = slice(D * s + N * (b - 1), D * s + N * (b + 1))
+                        nc.sync.dma_start(out=c_out[:, cols], in_=u_sb[:, cols])
+
+            xzbs = x_gate(1)
+            pending = None
+            for b in range(NB):
+                z_forget = []
+                for s in range(S):
+                    acc = new_acc()
+                    for g in range(G):
+                        h_pass(acc, s, 1, g, N * b, N)
+                    z = gate(acc, xzbs[b], 0, N)
+                    forget_product(s, b, z)
+                    z_forget.append(z)
+                if pending is not None:
+                    new_state(*pending)
+                pending = (b, z_forget)
+
+            xzbs = x_gate(2)
+            new_state(*pending)
+
+            def out_product(s, b, off, n, z):
+                ht = h_tiles[b // 2, s]
+                at = N * (b % 2) + off
+                nc.vector.tensor_tensor(out=ht[:, at : at + n], in0=z[:, 0:n], in1=ht[:, at : at + n], op=ALU.mult)
+                if b == 1:
+                    nc.sync.dma_start(out=h_out[:, D * s : D * s + 2 * N], in_=ht[:])
+                elif b >= 2:
+                    to = D * s + N * b + off
+                    nc.sync.dma_start(out=h_out[:, to : to + n], in_=ht[:, at : at + n])
+
+            pending = None
+            for b in range(NB):
+                for s in range(S):
+                    last = b == NB - 1 and s == S - 1
+                    for off, n in ((0, N // 2), (N // 2, N // 2)) if last else ((0, N),):
+                        acc = new_acc()
+                        for g in range(G):
+                            h_pass(acc, s, 2, g, N * b + off, n)
+                        z = gate(acc, xzbs[b], off, n)
+                        if pending is not None:
+                            out_product(*pending)
+                        pending = (s, b, off, n, z)
+            out_product(*pending)

@@ -15,6 +15,8 @@ G = D // 512
 N = 512
 NB = D // N
 
+I, F, O = range(3)
+
 FLOPS = 2 * (B + B * S) * D * 3 * D
 
 
@@ -23,6 +25,8 @@ def tile_rlstmcell_pb_kernel(
 ):
     nc = tc.nc
     c_upd = c_upd.rearrange("b s d -> b (s d)")
+    h_out_3d = h_out.rearrange("b (s d) -> b s d", s=S)
+    c_out_3d = c_out.rearrange("b (s d) -> b s d", s=S)
 
     with (
         tc.tile_pool(name="keep", bufs=1) as keep,
@@ -38,34 +42,44 @@ def tile_rlstmcell_pb_kernel(
         h_raw_planes = u8_tile("h_raw_planes", [P, G, S * B])
         h_codes = u8_tile("h_codes", [P, S, G, 2 * B])
         h_planes = u8_tile("h_planes", [P, S, G, B])
-        w_codes = {(m, a): u8_tile(f"{m}_codes_{a}", [P, G, 2 * D]) for m in "kr" for a in range(3)}
-        w_planes = {(m, a): u8_tile(f"{m}_planes_{a}", [P, G, D]) for m in "kr" for a in range(2)}
-        for m in "kr":
-            w_planes[m, 2] = w_planes[m, 0]
+
         w_src = {"k": (k_words, k_scales), "r": (r_words, r_scales)}
+        splits = {(m, a): [(0, D)] for m in "kr" for a in range(3)}
+        splits["r", O] = [(0, 2 * N), (2 * N, N), (3 * N, N)]
+        w_codes = {
+            (m, a): [(c0, n, u8_tile(f"{m}_codes_{a}_{c0}", [P, G, 2 * n])) for c0, n in parts]
+            for (m, a), parts in splits.items()
+            if (m, a) != ("k", O)
+        }
+        w_planes = {(m, a): u8_tile(f"{m}_planes_{a}", [P, G, D]) for m in "kr" for a in (F, I)}
+        for m in "kr":
+            w_planes[m, O] = w_planes[m, F]
+        w_codes["k", O] = w_codes["k", F]
 
         ident = keep.tile([P, P], BF16, name="ident")
         bias_rows = keep.tile([P, N], BF16, name="bias_rows")
         bias_sb = keep.tile([P, 3 * D], BF16, name="bias_sb")
-        cu_sb = keep.tile([P, S * D], BF16, name="cu_sb")
-        c_sb = keep.tile([P, S * D], BF16, name="c_sb")
-        u_sb = keep.tile([P, S * D], F32, name="u_sb")
+        cu_sb = keep.tile([P, S, D], BF16, name="cu_sb")
+        c_sb = keep.tile([P, S, D], BF16, name="c_sb")
+        cn = [keep.tile([P, S, N], F32, name=f"cn_{b}") for b in range(NB)]
         warm = keep.tile([P, 1], F32, name="warm")
 
-        def load_scales(planes, src, passes, cols):
-            for r in range(4):
+        def load_scales(planes, src, passes, cols, rows=range(4)):
+            for r in rows:
                 nc.sync.dma_start(
                     out=planes[r:P:32, passes, :].bitcast(I32),
                     in_=src[passes, r:16:4, cols].rearrange("g q n -> q g n").bitcast(I32),
                 )
 
-        def load_codes(m, a, p0, p1):
+        def load_codes(m, a, p0, p1, part=0):
+            c0, n, codes = w_codes[m, a][part]
+            c0 += D * a
             nc.sync.dma_start(
-                out=w_codes[m, a][:, p0:p1, :].bitcast(I32),
-                in_=w_src[m][0][p0:p1, :, 2 * D * a : 2 * D * (a + 1)].rearrange("g p n -> p g n").bitcast(I32),
+                out=codes[:, p0:p1, :].bitcast(I32),
+                in_=w_src[m][0][p0:p1, :, 2 * c0 : 2 * (c0 + n)].rearrange("g p n -> p g n").bitcast(I32),
             )
 
-        def load_w_scales(m, a, p0, p1):
+        def load_w_scales(m, a, p0=0, p1=G):
             load_scales(w_planes[m, a], w_src[m][1], slice(p0, p1), slice(D * a, D * (a + 1)))
 
         def zero(engine, ap):
@@ -76,11 +90,14 @@ def tile_rlstmcell_pb_kernel(
             return acc
 
         def mm(acc_ap, lhs, lhs_scale, m, a, g, c0, n):
+            for t0, tn, codes in w_codes[m, a]:
+                if t0 <= c0 < t0 + tn:
+                    rhs = codes[:, g, 2 * (c0 - t0) : 2 * (c0 - t0 + n)]
             nc.tensor.matmul_mx(
                 out=acc_ap,
                 lhsT=lhs.bitcast(FP4X4),
                 lhsT_scale=lhs_scale,
-                rhs=w_codes[m, a][:, g, 2 * c0 : 2 * (c0 + n)].bitcast(FP4X4),
+                rhs=rhs.bitcast(FP4X4),
                 rhs_scale=w_planes[m, a][:, g, c0 : c0 + n],
                 start=(g == 0),
                 stop=(g == G - 1),
@@ -92,10 +109,13 @@ def tile_rlstmcell_pb_kernel(
         def h_pass(acc, s, a, g, c0, n):
             mm(acc[:, 0:n], h_codes[:, s, g, :], h_planes[:, s, g, :], "r", a, g, c0, n)
 
-        def bias_spread(j):
+        def bias_spread(i, j):
             acc = new_acc()
             nc.tensor.matmul(acc[:], lhsT=ident[:, j : j + 1].to_broadcast([P, P]), rhs=bias_rows[:], start=True, stop=True)
-            nc.scalar.copy(out=bias_sb[:, N * j : N * (j + 1)], in_=acc[:])
+            if i % 2 == 0:
+                nc.scalar.copy(out=bias_sb[:, N * j : N * (j + 1)], in_=acc[:])
+            else:
+                nc.vector.tensor_copy(out=bias_sb[:, N * j : N * (j + 1)], in_=acc[:])
 
         def x_drain(acc, a, b):
             xzb = work.tile([P, N], F32, name="xzb", bufs=6)
@@ -103,57 +123,59 @@ def tile_rlstmcell_pb_kernel(
             nc.vector.tensor_tensor(out=xzb[:], in0=acc[:], in1=bias_sb[:, c0 : c0 + N], op=ALU.add)
             return xzb
 
-        def gate(acc, xzb, off, n):
-            z = work.tile([P, N], F32, name="z", bufs=8)
-            nc.vector.tensor_tensor(out=z[:, 0:n], in0=acc[:, 0:n], in1=xzb[:, off : off + n], op=ALU.add)
-            nc.scalar.activation(out=z[:, 0:n], in_=z[:, 0:n], func=ACT.Sigmoid)
+        def new_z():
+            z = work.tile([P, S, N], F32, name="z", bufs=7)
             return z
 
-        def state_cols(s, b):
-            return slice(D * s + N * b, D * s + N * (b + 1))
+        def z_add(z, s, acc, xzb, off=0, n=N):
+            at = slice(off, off + n)
+            nc.vector.tensor_tensor(out=z[:, s, at], in0=acc[:, 0:n], in1=xzb[:, at], op=ALU.add)
+
+        def act(out, in_, func):
+            nc.scalar.activation(out=out, in_=in_, func=func)
+
+        def blk(b):
+            return slice(N * b, N * (b + 1))
 
         with tc.manual_schedule():
             nc.vector.memset(warm[:], 0.0)
             zero(nc.vector, x_planes[:])
-            zero(nc.vector, w_planes["k", 0][:, 0, :])
             nc.vector.memset(bias_rows[:], 0.0)
-            zero(nc.vector, w_planes["k", 0][:, 1:G, :])
+            zero(nc.vector, w_planes["k", F][:, 0:2, :])
             zero(nc.vector, h_raw_planes[:])
-            nc.scalar.activation(out=warm[:], in_=warm[:], func=ACT.Sigmoid)
-            make_identity(nc, ident[:])
+            zero(nc.gpsimd, w_planes["k", F][:, 2:G, :])
             nc.gpsimd.dma_start(out=bias_rows[0:12, :], in_=bias.rearrange("(j n) -> j n", n=N))
-            for m, a in (("r", 0), ("k", 1), ("r", 1)):
-                zero(nc.gpsimd, w_planes[m, a][:])
+            make_identity(nc, ident[:])
+            act(warm[:], warm[:], ACT.Sigmoid)
+            for m, a in (("r", F), ("k", I), ("r", I)):
+                for g in range(G):
+                    zero(nc.gpsimd, w_planes[m, a][:, g, :])
+            for i in range(2 * NB):
+                bias_spread(i, NB * (F, I)[i // NB] + i % NB)
 
             nc.sync.dma_start(out=x_codes[:].bitcast(I32), in_=x_words.rearrange("g p n -> p g n").bitcast(I32))
-            load_codes("k", 0, 0, 1)
-            load_scales(x_planes, x_scales, slice(0, G), slice(0, B))
-            load_w_scales("k", 0, 0, 1)
-            load_codes("k", 0, 1, 2)
+            load_scales(x_planes, x_scales, slice(0, G), slice(0, B), range(0, 2))
+            load_codes("k", F, 0, 1)
+            load_scales(x_planes, x_scales, slice(0, G), slice(0, B), range(2, 4))
+            load_w_scales("k", F)
+            load_codes("k", F, 1, 2)
+            load_codes("k", F, 2, 3)
             nc.sync.dma_start(out=h_raw[:].bitcast(I32), in_=h_words.rearrange("g p n -> p g n").bitcast(I32))
-            load_w_scales("k", 0, 1, G)
-            load_codes("k", 0, 2, 3)
-            load_codes("k", 0, 3, 4)
             load_scales(h_raw_planes, h_scales, slice(0, G), slice(0, S * B))
-            load_codes("r", 0, 0, 1)
-            load_w_scales("r", 0, 0, G)
-            load_codes("r", 0, 1, 2)
-            load_codes("r", 0, 2, 3)
-            load_codes("r", 0, 3, 4)
+            load_codes("k", F, 3, 4)
+            load_w_scales("r", F)
+            for g in range(G):
+                load_codes("r", F, g, g + 1)
+            load_w_scales("k", I)
+            load_codes("k", I, 0, 2)
+            load_codes("k", I, 2, 4)
+            load_w_scales("r", I)
+            load_codes("r", I, 0, 2)
+            load_codes("r", I, 2, 4)
             for s in range(S):
-                nc.sync.dma_start(out=cu_sb[:, D * s : D * (s + 1)], in_=c_upd[:, D * s : D * (s + 1)])
-            def load_gate(a):
-                for m in "kr":
-                    load_codes(m, a, 0, 2)
-                    load_w_scales(m, a, 0, G)
-                    load_codes(m, a, 2, 4)
-
-            load_gate(1)
+                nc.sync.dma_start(out=c_sb[:, s, :], in_=c_state[:, D * s : D * (s + 1)])
             for s in range(S):
-                nc.sync.dma_start(out=c_sb[:, D * s : D * (s + 1)], in_=c_state[:, D * s : D * (s + 1)])
-
-            for j in range(NB):
-                bias_spread(j)
+                nc.sync.dma_start(out=cu_sb[:, s, :], in_=c_upd[:, D * s : D * (s + 1)])
 
             for s in range(S):
                 nc.vector.tensor_copy(
@@ -166,39 +188,29 @@ def tile_rlstmcell_pb_kernel(
                     in_=h_raw_planes[:].rearrange("p g (b s) -> p g b s", s=S)[:, :, :, s],
                 )
 
-            def u_chunk(s, half):
-                cols = slice(D * s + D // 2 * half, D * s + D // 2 * (half + 1))
-                nc.scalar.activation(out=u_sb[:, cols], in_=cu_sb[:, cols], func=ACT.Tanh)
-
-            def in_product(s, b, z):
-                cols = state_cols(s, b)
-                nc.gpsimd.tensor_tensor(out=u_sb[:, cols], in0=z[:], in1=u_sb[:, cols], op=ALU.mult)
-
-            def forget_product(s, b, z):
-                nc.gpsimd.tensor_tensor(out=z[:], in0=z[:], in1=c_sb[:, state_cols(s, b)], op=ALU.mult)
+            def h_unit(a, b, xzb):
+                z = new_z()
+                accs = [new_acc() for s in range(S)]
+                for g in range(G):
+                    for s in range(S):
+                        h_pass(accs[s], s, a, g, N * b, N)
+                for s in range(S):
+                    z_add(z, s, accs[s], xzb)
+                return z
 
             accs = [new_acc() for b in range(NB)]
             for g in range(G):
                 for b in range(NB):
-                    x_pass(accs[b], 0, b, g)
-            xzbs = [x_drain(accs[b], 0, b) for b in range(NB)]
-            for j in range(NB, 3 * NB):
-                bias_spread(j)
-            z_in = {}
-            for half in range(2):
-                units = [(b, s) for b in (2 * half, 2 * half + 1) for s in range(S)]
-                accs = {unit: new_acc() for unit in units}
-                for g in range(G):
-                    for b, s in units:
-                        h_pass(accs[b, s], s, 0, g, N * b, N)
-                for b, s in units:
-                    z_in[b, s] = gate(accs[b, s], xzbs[b], 0, N)
-                for s in range(S):
-                    u_chunk(s, half)
-                for b, s in units:
-                    in_product(s, b, z_in[b, s])
+                    x_pass(accs[b], F, b, g)
+            for j in range(NB):
+                bias_spread(j, NB * O + j)
+            xzbs = [x_drain(accs[b], F, b) for b in range(NB)]
+            forgets = []
+            states = []
 
-            load_gate(2)
+            def new_state(b, z):
+                nc.vector.tensor_tensor(out=cn[b][:], in0=z[:], in1=cn[b][:], op=ALU.add)
+                nc.sync.dma_start(out=c_out_3d[:, :, blk(b)], in_=cn[b][:])
 
             def x_gate(a):
                 out = []
@@ -209,61 +221,62 @@ def tile_rlstmcell_pb_kernel(
                     out.append(x_drain(acc, a, b))
                 return out
 
-            h_tiles = {}
+            def forget_product(b, z):
+                nc.vector.tensor_tensor(out=cn[b][:], in0=z[:], in1=c_sb[:, :, blk(b)], op=ALU.mult)
 
-            def new_state(b, z_forget):
-                for s in range(S):
-                    cols = state_cols(s, b)
-                    nc.vector.tensor_tensor(out=u_sb[:, cols], in0=z_forget[s][:], in1=u_sb[:, cols], op=ALU.add)
-                for s in range(S):
-                    if b % 2 == 0:
-                        ht = work.tile([P, 2 * N], F32, name="ht", bufs=4)
-                        h_tiles[b // 2, s] = ht
-                    nc.scalar.activation(
-                        out=h_tiles[b // 2, s][:, N * (b % 2) : N * (b % 2 + 1)], in_=u_sb[:, state_cols(s, b)], func=ACT.Tanh
-                    )
-                    if b % 2 == 1:
-                        cols = slice(D * s + N * (b - 1), D * s + N * (b + 1))
-                        nc.sync.dma_start(out=c_out[:, cols], in_=u_sb[:, cols])
-
-            xzbs = x_gate(1)
-            pending = None
             for b in range(NB):
-                z_forget = []
-                for s in range(S):
-                    acc = new_acc()
-                    for g in range(G):
-                        h_pass(acc, s, 1, g, N * b, N)
-                    z = gate(acc, xzbs[b], 0, N)
-                    forget_product(s, b, z)
-                    z_forget.append(z)
-                if pending is not None:
-                    new_state(*pending)
-                pending = (b, z_forget)
+                z = h_unit(F, b, xzbs[b])
+                act(z[:], z[:], ACT.Sigmoid)
+                forgets.append((b, z))
 
-            xzbs = x_gate(2)
-            new_state(*pending)
+            load_w_scales("k", O)
+            load_w_scales("r", O)
+            load_codes("k", O, 0, 2)
+            load_codes("k", O, 2, 4)
+            for part in range(3):
+                load_codes("r", O, 0, G, part)
 
-            def out_product(s, b, off, n, z):
-                ht = h_tiles[b // 2, s]
-                at = N * (b % 2) + off
-                nc.vector.tensor_tensor(out=ht[:, at : at + n], in0=z[:, 0:n], in1=ht[:, at : at + n], op=ALU.mult)
-                if b == 1:
-                    nc.sync.dma_start(out=h_out[:, D * s : D * s + 2 * N], in_=ht[:])
-                elif b >= 2:
-                    to = D * s + N * b + off
-                    nc.sync.dma_start(out=h_out[:, to : to + n], in_=ht[:, at : at + n])
-
-            pending = None
+            xzbs = x_gate(I)
             for b in range(NB):
+                z = h_unit(I, b, xzbs[b])
+                u = work.tile([P, S, N], F32, name="u", bufs=3)
+                for forget in forgets[2 * b : 2 * b + 2]:
+                    forget_product(*forget)
+                act(u[:], cu_sb[:, :, blk(b)], ACT.Tanh)
+                act(z[:], z[:], ACT.Sigmoid)
                 for s in range(S):
-                    last = b == NB - 1 and s == S - 1
-                    for off, n in ((0, N // 2), (N // 2, N // 2)) if last else ((0, N),):
+                    nc.gpsimd.tensor_tensor(out=z[:, s, :], in0=z[:, s, :], in1=u[:, s, :], op=ALU.mult)
+                states.append((b, z))
+                if len(states) > 2:
+                    new_state(*states.pop(0))
+
+            xzbs = x_gate(O)
+            pending = []
+
+            def out_product(b, ht, z, s0, s1, off, n):
+                at = slice(off, off + n)
+                nc.vector.tensor_tensor(out=ht[:, s0:s1, at], in0=z[:, s0:s1, at], in1=ht[:, s0:s1, at], op=ALU.mult)
+                nc.sync.dma_start(out=h_out_3d[:, s0:s1, N * b + off : N * b + off + n], in_=ht[:, s0:s1, at])
+
+            for b in range(NB):
+                ht = work.tile([P, S, N], F32, name="ht", bufs=4)
+                act(ht[:], cn[b][:], ACT.Tanh)
+                if b < NB - 1:
+                    z = h_unit(O, b, xzbs[b])
+                    act(z[:], z[:], ACT.Sigmoid)
+                    if states:
+                        new_state(*states.pop(0))
+                    if pending:
+                        out_product(*pending.pop())
+                    pending.append((b, ht, z, 0, S, 0, N))
+                else:
+                    z = new_z()
+                    for s, off, n in ((0, 0, N), (1, 0, N // 2), (1, N // 2, N // 2)):
                         acc = new_acc()
                         for g in range(G):
-                            h_pass(acc, s, 2, g, N * b + off, n)
-                        z = gate(acc, xzbs[b], off, n)
-                        if pending is not None:
-                            out_product(*pending)
-                        pending = (s, b, off, n, z)
-            out_product(*pending)
+                            h_pass(acc, s, O, g, N * b + off, n)
+                        z_add(z, s, acc, xzbs[b], off, n)
+                        act(z[:, s, off : off + n], z[:, s, off : off + n], ACT.Sigmoid)
+                        out_product(*pending.pop())
+                        pending.append((b, ht, z, s, s + 1, off, n))
+            out_product(*pending.pop())

@@ -24,7 +24,7 @@ def tile_rlstmcell_pb_kernel(
     tc, x_words, x_scales, h_words, h_scales, c_state, c_upd, k_words, k_scales, r_words, r_scales, bias, h_out, c_out
 ):
     nc = tc.nc
-    c_upd = c_upd.rearrange("b s d -> b (s d)")
+    c_state = c_state.rearrange("b (s d) -> b s d", s=S)
     h_out_3d = h_out.rearrange("b (s d) -> b s d", s=S)
     c_out_3d = c_out.rearrange("b (s d) -> b s d", s=S)
 
@@ -44,23 +44,27 @@ def tile_rlstmcell_pb_kernel(
         h_planes = u8_tile("h_planes", [P, S, G, B])
 
         w_src = {"k": (k_words, k_scales), "r": (r_words, r_scales)}
-        splits = {(m, a): [(0, D)] for m in "kr" for a in range(3)}
-        splits["r", O] = [(0, 2 * N), (2 * N, N), (3 * N, N)]
-        w_codes = {
-            (m, a): [(c0, n, u8_tile(f"{m}_codes_{a}_{c0}", [P, G, 2 * n])) for c0, n in parts]
-            for (m, a), parts in splits.items()
-            if (m, a) != ("k", O)
-        }
-        w_planes = {(m, a): u8_tile(f"{m}_planes_{a}", [P, G, D]) for m in "kr" for a in (F, I)}
+        w_codes = {}
+        for m, a, parts in (("k", I, 1), ("r", I, 2), ("k", F, 1), ("r", F, 2)):
+            n = D // parts
+            w_codes[m, a] = [(n * j, n, u8_tile(f"{m}_codes_{a}_{j}", [P, G, 2 * n])) for j in range(parts)]
         for m in "kr":
-            w_planes[m, O] = w_planes[m, F]
-        w_codes["k", O] = w_codes["k", F]
+            w_codes[m, O] = w_codes[m, I]
+
+        i_planes = {m: u8_tile(f"{m}_planes_i", [P, G, D]) for m in "kr"}
+        fo_planes = {m: u8_tile(f"{m}_planes_fo", [P, G, 2 * D]) for m in "kr"}
+
+        def scale_cols(m, a, g, c0, n):
+            if a == I:
+                return i_planes[m][:, g, c0 : c0 + n]
+            c0 += D * (a - F)
+            return fo_planes[m][:, g, c0 : c0 + n]
 
         ident = keep.tile([P, P], BF16, name="ident")
         bias_rows = keep.tile([P, N], BF16, name="bias_rows")
         bias_sb = keep.tile([P, 3 * D], BF16, name="bias_sb")
-        cu_sb = keep.tile([P, S, D], BF16, name="cu_sb")
-        c_sb = keep.tile([P, S, D], BF16, name="c_sb")
+        cu_sb = [keep.tile([P, S, 2 * N], BF16, name=f"cu_{j}") for j in range(2)]
+        c_sb = [keep.tile([P, S, 2 * N], BF16, name=f"c_{j}") for j in range(2)]
         cn = [keep.tile([P, S, N], F32, name=f"cn_{b}") for b in range(NB)]
         warm = keep.tile([P, 1], F32, name="warm")
 
@@ -79,8 +83,17 @@ def tile_rlstmcell_pb_kernel(
                 in_=w_src[m][0][p0:p1, :, 2 * c0 : 2 * (c0 + n)].rearrange("g p n -> p g n").bitcast(I32),
             )
 
-        def load_w_scales(m, a, p0=0, p1=G):
-            load_scales(w_planes[m, a], w_src[m][1], slice(p0, p1), slice(D * a, D * (a + 1)))
+        def load_i_scales(m):
+            load_scales(i_planes[m], w_src[m][1], slice(0, G), slice(0, D))
+
+        def load_fo_scales(m):
+            load_scales(fo_planes[m], w_src[m][1], slice(0, G), slice(D * F, 3 * D))
+
+        def load_half(tiles, src, j):
+            nc.sync.dma_start(out=tiles[j][:], in_=src[:, :, 2 * N * j : 2 * N * (j + 1)])
+
+        def half_block(tiles, b):
+            return tiles[b // 2][:, :, N * (b % 2) : N * (b % 2 + 1)]
 
         def zero(engine, ap):
             engine.memset(ap.bitcast(I32), 0)
@@ -98,7 +111,7 @@ def tile_rlstmcell_pb_kernel(
                 lhsT=lhs.bitcast(FP4X4),
                 lhsT_scale=lhs_scale,
                 rhs=rhs.bitcast(FP4X4),
-                rhs_scale=w_planes[m, a][:, g, c0 : c0 + n],
+                rhs_scale=scale_cols(m, a, g, c0, n),
                 start=(g == 0),
                 stop=(g == G - 1),
             )
@@ -124,7 +137,7 @@ def tile_rlstmcell_pb_kernel(
             return xzb
 
         def new_z():
-            z = work.tile([P, S, N], F32, name="z", bufs=7)
+            z = work.tile([P, S, N], F32, name="z", bufs=8)
             return z
 
         def z_add(z, s, acc, xzb, off=0, n=N):
@@ -141,41 +154,45 @@ def tile_rlstmcell_pb_kernel(
             nc.vector.memset(warm[:], 0.0)
             zero(nc.vector, x_planes[:])
             nc.vector.memset(bias_rows[:], 0.0)
-            zero(nc.vector, w_planes["k", F][:, 0:2, :])
+            zero(nc.vector, i_planes["k"][:, 0:2, :])
             zero(nc.vector, h_raw_planes[:])
-            zero(nc.gpsimd, w_planes["k", F][:, 2:G, :])
+            zero(nc.gpsimd, i_planes["k"][:, 2:G, :])
             nc.gpsimd.dma_start(out=bias_rows[0:12, :], in_=bias.rearrange("(j n) -> j n", n=N))
             make_identity(nc, ident[:])
             act(warm[:], warm[:], ACT.Sigmoid)
-            for m, a in (("r", F), ("k", I), ("r", I)):
+            for g in range(G):
+                zero(nc.gpsimd, i_planes["r"][:, g, :])
+            for m in "kr":
                 for g in range(G):
-                    zero(nc.gpsimd, w_planes[m, a][:, g, :])
+                    zero(nc.gpsimd, fo_planes[m][:, g, :])
             for i in range(2 * NB):
-                bias_spread(i, NB * (F, I)[i // NB] + i % NB)
+                bias_spread(i, NB * (I, F)[i // NB] + i % NB)
 
             nc.sync.dma_start(out=x_codes[:].bitcast(I32), in_=x_words.rearrange("g p n -> p g n").bitcast(I32))
             load_scales(x_planes, x_scales, slice(0, G), slice(0, B), range(0, 2))
-            load_codes("k", F, 0, 1)
+            load_codes("k", I, 0, 1)
             load_scales(x_planes, x_scales, slice(0, G), slice(0, B), range(2, 4))
-            load_w_scales("k", F)
-            load_codes("k", F, 1, 2)
-            load_codes("k", F, 2, 3)
+            load_i_scales("k")
+            load_codes("k", I, 1, 2)
+            load_codes("k", I, 2, 3)
             nc.sync.dma_start(out=h_raw[:].bitcast(I32), in_=h_words.rearrange("g p n -> p g n").bitcast(I32))
             load_scales(h_raw_planes, h_scales, slice(0, G), slice(0, S * B))
-            load_codes("k", F, 3, 4)
-            load_w_scales("r", F)
-            for g in range(G):
-                load_codes("r", F, g, g + 1)
-            load_w_scales("k", I)
-            load_codes("k", I, 0, 2)
-            load_codes("k", I, 2, 4)
-            load_w_scales("r", I)
-            load_codes("r", I, 0, 2)
-            load_codes("r", I, 2, 4)
-            for s in range(S):
-                nc.sync.dma_start(out=c_sb[:, s, :], in_=c_state[:, D * s : D * (s + 1)])
-            for s in range(S):
-                nc.sync.dma_start(out=cu_sb[:, s, :], in_=c_upd[:, D * s : D * (s + 1)])
+            load_codes("k", I, 3, 4)
+            load_i_scales("r")
+            load_half(cu_sb, c_upd, 0)
+            load_codes("r", I, 0, 2, 0)
+            load_codes("r", I, 2, 4, 0)
+            load_half(cu_sb, c_upd, 1)
+            load_codes("r", I, 0, 2, 1)
+            load_codes("r", I, 2, 4, 1)
+            load_fo_scales("k")
+            load_fo_scales("r")
+            load_codes("k", F, 0, 2)
+            load_codes("k", F, 2, 4)
+            for half in range(2):
+                load_half(c_sb, c_state, half)
+                load_codes("r", F, 0, 2, half)
+                load_codes("r", F, 2, 4, half)
 
             for s in range(S):
                 nc.vector.tensor_copy(
@@ -201,56 +218,75 @@ def tile_rlstmcell_pb_kernel(
             accs = [new_acc() for b in range(NB)]
             for g in range(G):
                 for b in range(NB):
-                    x_pass(accs[b], F, b, g)
+                    x_pass(accs[b], I, b, g)
             for j in range(NB):
                 bias_spread(j, NB * O + j)
-            xzbs = [x_drain(accs[b], F, b) for b in range(NB)]
-            forgets = []
-            states = []
+            xzbs = [x_drain(accs[b], I, b) for b in range(NB)]
+            inputs = []
+            h_tiles = []
 
             def new_state(b, z):
                 nc.vector.tensor_tensor(out=cn[b][:], in0=z[:], in1=cn[b][:], op=ALU.add)
+                ht = work.tile([P, S, N], F32, name="ht", bufs=4)
+                act(ht[:], cn[b][:], ACT.Tanh)
+                h_tiles.append(ht)
                 nc.sync.dma_start(out=c_out_3d[:, :, blk(b)], in_=cn[b][:])
 
-            def x_gate(a):
+            def x_gate(a, between=()):
                 out = []
                 for b in range(NB):
                     acc = new_acc()
                     for g in range(G):
                         x_pass(acc, a, b, g)
                     out.append(x_drain(acc, a, b))
+                    for step in between[b : b + 1]:
+                        step()
                 return out
 
-            def forget_product(b, z):
-                nc.vector.tensor_tensor(out=cn[b][:], in0=z[:], in1=c_sb[:, :, blk(b)], op=ALU.mult)
+            def forget_product(engine, b, s, z):
+                engine.tensor_tensor(out=z[:, s, :], in0=z[:, s, :], in1=half_block(c_sb, b)[:, s, :], op=ALU.mult)
 
-            for b in range(NB):
-                z = h_unit(F, b, xzbs[b])
-                act(z[:], z[:], ACT.Sigmoid)
-                forgets.append((b, z))
+            def in_product(b, z):
+                nc.vector.tensor_tensor(out=cn[b][:], in0=z[:], in1=cn[b][:], op=ALU.mult)
 
-            load_w_scales("k", O)
-            load_w_scales("r", O)
-            load_codes("k", O, 0, 2)
-            load_codes("k", O, 2, 4)
-            for part in range(3):
-                load_codes("r", O, 0, G, part)
-
-            xzbs = x_gate(I)
             for b in range(NB):
                 z = h_unit(I, b, xzbs[b])
-                u = work.tile([P, S, N], F32, name="u", bufs=3)
-                for forget in forgets[2 * b : 2 * b + 2]:
-                    forget_product(*forget)
-                act(u[:], cu_sb[:, :, blk(b)], ACT.Tanh)
+                act(cn[b][:], half_block(cu_sb, b), ACT.Tanh)
                 act(z[:], z[:], ACT.Sigmoid)
-                for s in range(S):
-                    nc.gpsimd.tensor_tensor(out=z[:, s, :], in0=z[:, s, :], in1=u[:, s, :], op=ALU.mult)
-                states.append((b, z))
-                if len(states) > 2:
-                    new_state(*states.pop(0))
+                if inputs:
+                    in_product(*inputs.pop())
+                inputs.append((b, z))
 
-            xzbs = x_gate(O)
+            load_codes("k", O, 0, 2)
+            load_codes("k", O, 2, 4)
+            for part in range(2):
+                for g in (0, 2):
+                    load_codes("r", O, g, g + 2, part)
+
+            xzbs = x_gate(F)
+            zs = []
+            for b in range(NB):
+                z = h_unit(F, b, xzbs[b])
+                zs.append(z)
+                act(z[:], z[:], ACT.Sigmoid)
+                forget_product(nc.gpsimd, b, 0, z)
+                if b % 2 == 0:
+                    forget_product(nc.gpsimd, b, 1, z)
+                if b == 0:
+                    in_product(*inputs.pop())
+                elif b == 2:
+                    forget_product(nc.vector, 1, 1, zs[1])
+                    new_state(0, zs[0])
+                elif b == 3:
+                    new_state(1, zs[1])
+
+            between = (
+                lambda: forget_product(nc.vector, 3, 1, zs[3]),
+                lambda: new_state(2, zs[2]),
+                lambda: None,
+                lambda: new_state(3, zs[3]),
+            )
+            xzbs = x_gate(O, between)
             pending = []
 
             def out_product(b, ht, z, s0, s1, off, n):
@@ -259,13 +295,10 @@ def tile_rlstmcell_pb_kernel(
                 nc.sync.dma_start(out=h_out_3d[:, s0:s1, N * b + off : N * b + off + n], in_=ht[:, s0:s1, at])
 
             for b in range(NB):
-                ht = work.tile([P, S, N], F32, name="ht", bufs=4)
-                act(ht[:], cn[b][:], ACT.Tanh)
+                ht = h_tiles[b]
                 if b < NB - 1:
                     z = h_unit(O, b, xzbs[b])
                     act(z[:], z[:], ACT.Sigmoid)
-                    if states:
-                        new_state(*states.pop(0))
                     if pending:
                         out_product(*pending.pop())
                     pending.append((b, ht, z, 0, S, 0, N))

@@ -1,3 +1,5 @@
+from functools import partial
+
 import concourse.mybir as mybir
 from concourse.masks import make_identity
 
@@ -17,6 +19,10 @@ NB = D // N
 
 I, F, O = range(3)
 
+NBIAS = 384
+
+ROW_PARTS = (slice(0, 4), slice(4, 112), slice(112, P))
+
 FLOPS = 2 * (B + B * S) * D * 3 * D
 
 
@@ -24,9 +30,8 @@ def tile_rlstmcell_pb_kernel(
     tc, x_words, x_scales, h_words, h_scales, c_state, c_upd, k_words, k_scales, r_words, r_scales, bias, h_out, c_out
 ):
     nc = tc.nc
-    c_state = c_state.rearrange("b (s d) -> b s d", s=S)
-    h_out_3d = h_out.rearrange("b (s d) -> b s d", s=S)
-    c_out_3d = c_out.rearrange("b (s d) -> b s d", s=S)
+    c_upd = c_upd.rearrange("b s d -> b (s d)")
+    h_out = h_out.rearrange("b (s d) -> b s d", s=S)
 
     with (
         tc.tile_pool(name="keep", bufs=1) as keep,
@@ -42,58 +47,50 @@ def tile_rlstmcell_pb_kernel(
         h_raw_planes = u8_tile("h_raw_planes", [P, G, S * B])
         h_codes = u8_tile("h_codes", [P, S, G, 2 * B])
         h_planes = u8_tile("h_planes", [P, S, G, B])
-
-        w_src = {"k": (k_words, k_scales), "r": (r_words, r_scales)}
-        w_codes = {}
-        for m, a, parts in (("k", I, 1), ("r", I, 2), ("k", F, 1), ("r", F, 2)):
-            n = D // parts
-            w_codes[m, a] = [(n * j, n, u8_tile(f"{m}_codes_{a}_{j}", [P, G, 2 * n])) for j in range(parts)]
+        w_codes = {(m, a): u8_tile(f"{m}_codes_{a}", [P, G, 2 * D]) for m in "kr" for a in (I, F)}
+        w_planes = {(m, a): u8_tile(f"{m}_planes_{a}", [P, G, D]) for m in "kr" for a in (I, F)}
         for m in "kr":
-            w_codes[m, O] = w_codes[m, I]
+            w_planes[m, O] = w_planes[m, I]
+        w_codes["k", O] = w_codes["k", I]
+        r_flat = w_codes["r", I][:].rearrange("p g n -> p (g n)")
+        r_o_codes = [r_flat[:, 4 * D * j : 4 * D * (j + 1)].rearrange("p (g n) -> p g n", g=G) for j in range(2)]
 
-        i_planes = {m: u8_tile(f"{m}_planes_i", [P, G, D]) for m in "kr"}
-        fo_planes = {m: u8_tile(f"{m}_planes_fo", [P, G, 2 * D]) for m in "kr"}
-
-        def scale_cols(m, a, g, c0, n):
-            if a == I:
-                return i_planes[m][:, g, c0 : c0 + n]
-            c0 += D * (a - F)
-            return fo_planes[m][:, g, c0 : c0 + n]
+        def operand(m, a, g, c0, n):
+            if (m, a) == ("r", O):
+                at = 2 * (c0 % (2 * N))
+                codes = r_o_codes[c0 // (2 * N)][:, g, at : at + 2 * n]
+            else:
+                codes = w_codes[m, a][:, g, 2 * c0 : 2 * (c0 + n)]
+            return codes, w_planes[m, a][:, g, c0 : c0 + n]
 
         ident = keep.tile([P, P], BF16, name="ident")
-        bias_rows = keep.tile([P, N], BF16, name="bias_rows")
+        bias_rows = keep.tile([P, NBIAS], BF16, name="bias_rows")
         bias_sb = keep.tile([P, 3 * D], BF16, name="bias_sb")
-        cu_sb = [keep.tile([P, S, 2 * N], BF16, name=f"cu_{j}") for j in range(2)]
-        c_sb = [keep.tile([P, S, 2 * N], BF16, name=f"c_{j}") for j in range(2)]
-        cn = [keep.tile([P, S, N], F32, name=f"cn_{b}") for b in range(NB)]
+        cu_sb = keep.tile([P, S, D], BF16, name="cu_sb")
+        c_sb = keep.tile([P, S, D], BF16, name="c_sb")
+        cn = keep.tile([P, S, D], F32, name="cn")
+        ht = keep.tile([P, S, D], F32, name="ht")
         warm = keep.tile([P, 1], F32, name="warm")
 
-        def load_scales(planes, src, passes, cols, rows=range(4)):
+        def blk(b):
+            return slice(N * b, N * (b + 1))
+
+        def load_scales(planes, src, c0, n, rows=range(4)):
             for r in rows:
                 nc.sync.dma_start(
-                    out=planes[r:P:32, passes, :].bitcast(I32),
-                    in_=src[passes, r:16:4, cols].rearrange("g q n -> q g n").bitcast(I32),
+                    out=planes[r:P:32, :, :].bitcast(I32),
+                    in_=src[:, r:16:4, c0 : c0 + n].rearrange("g q n -> q g n").bitcast(I32),
                 )
 
-        def load_codes(m, a, p0, p1, part=0):
-            c0, n, codes = w_codes[m, a][part]
-            c0 += D * a
+        def load_codes(codes, src, p0, p1, c0, n):
             nc.sync.dma_start(
-                out=codes[:, p0:p1, :].bitcast(I32),
-                in_=w_src[m][0][p0:p1, :, 2 * c0 : 2 * (c0 + n)].rearrange("g p n -> p g n").bitcast(I32),
+                out=codes.bitcast(I32),
+                in_=src[p0:p1, :, 2 * c0 : 2 * (c0 + n)].rearrange("g p n -> p g n").bitcast(I32),
             )
 
-        def load_i_scales(m):
-            load_scales(i_planes[m], w_src[m][1], slice(0, G), slice(0, D))
-
-        def load_fo_scales(m):
-            load_scales(fo_planes[m], w_src[m][1], slice(0, G), slice(D * F, 3 * D))
-
-        def load_half(tiles, src, j):
-            nc.sync.dma_start(out=tiles[j][:], in_=src[:, :, 2 * N * j : 2 * N * (j + 1)])
-
-        def half_block(tiles, b):
-            return tiles[b // 2][:, :, N * (b % 2) : N * (b % 2 + 1)]
+        def pool_dma(out, in_):
+            for rows in ROW_PARTS:
+                nc.gpsimd.dma_start(out=out[rows], in_=in_[rows])
 
         def zero(engine, ap):
             engine.memset(ap.bitcast(I32), 0)
@@ -102,42 +99,42 @@ def tile_rlstmcell_pb_kernel(
             acc = psum.tile([P, N], F32, name="acc")
             return acc
 
-        def mm(acc_ap, lhs, lhs_scale, m, a, g, c0, n):
-            for t0, tn, codes in w_codes[m, a]:
-                if t0 <= c0 < t0 + tn:
-                    rhs = codes[:, g, 2 * (c0 - t0) : 2 * (c0 - t0 + n)]
+        def mm(acc_ap, lhs, lhs_scale, rhs, g):
             nc.tensor.matmul_mx(
                 out=acc_ap,
                 lhsT=lhs.bitcast(FP4X4),
                 lhsT_scale=lhs_scale,
-                rhs=rhs.bitcast(FP4X4),
-                rhs_scale=scale_cols(m, a, g, c0, n),
+                rhs=rhs[0].bitcast(FP4X4),
+                rhs_scale=rhs[1],
                 start=(g == 0),
                 stop=(g == G - 1),
             )
 
         def x_pass(acc, a, b, g):
-            mm(acc[:], x_codes[:, g, :], x_planes[:, g, :], "k", a, g, N * b, N)
+            mm(acc[:], x_codes[:, g, :], x_planes[:, g, :], operand("k", a, g, N * b, N), g)
 
         def h_pass(acc, s, a, g, c0, n):
-            mm(acc[:, 0:n], h_codes[:, s, g, :], h_planes[:, s, g, :], "r", a, g, c0, n)
+            mm(acc[:, 0:n], h_codes[:, s, g, :], h_planes[:, s, g, :], operand("r", a, g, c0, n), g)
 
-        def bias_spread(i, j):
+        def bias_spread(j):
             acc = new_acc()
-            nc.tensor.matmul(acc[:], lhsT=ident[:, j : j + 1].to_broadcast([P, P]), rhs=bias_rows[:], start=True, stop=True)
-            if i % 2 == 0:
-                nc.scalar.copy(out=bias_sb[:, N * j : N * (j + 1)], in_=acc[:])
+            nc.tensor.matmul(
+                acc[:, 0:NBIAS], lhsT=ident[:, j : j + 1].to_broadcast([P, P]), rhs=bias_rows[:], start=True, stop=True
+            )
+            out = bias_sb[:, NBIAS * j : NBIAS * (j + 1)]
+            if j % 2 == 0:
+                nc.scalar.copy(out=out, in_=acc[:, 0:NBIAS])
             else:
-                nc.vector.tensor_copy(out=bias_sb[:, N * j : N * (j + 1)], in_=acc[:])
+                nc.vector.tensor_copy(out=out, in_=acc[:, 0:NBIAS])
 
         def x_drain(acc, a, b):
-            xzb = work.tile([P, N], F32, name="xzb", bufs=6)
+            xzb = work.tile([P, N], F32, name="xzb", bufs=8)
             c0 = D * a + N * b
             nc.vector.tensor_tensor(out=xzb[:], in0=acc[:], in1=bias_sb[:, c0 : c0 + N], op=ALU.add)
             return xzb
 
         def new_z():
-            z = work.tile([P, S, N], F32, name="z", bufs=8)
+            z = work.tile([P, S, N], F32, name="z", bufs=6)
             return z
 
         def z_add(z, s, acc, xzb, off=0, n=N):
@@ -147,52 +144,53 @@ def tile_rlstmcell_pb_kernel(
         def act(out, in_, func):
             nc.scalar.activation(out=out, in_=in_, func=func)
 
-        def blk(b):
-            return slice(N * b, N * (b + 1))
+        def mul(engine, out, in0, in1):
+            engine.tensor_tensor(out=out, in0=in0, in1=in1, op=ALU.mult)
 
         with tc.manual_schedule():
             nc.vector.memset(warm[:], 0.0)
             zero(nc.vector, x_planes[:])
             nc.vector.memset(bias_rows[:], 0.0)
-            zero(nc.vector, i_planes["k"][:, 0:2, :])
+            zero(nc.vector, w_planes["k", I][:, 0:2, :])
             zero(nc.vector, h_raw_planes[:])
-            zero(nc.gpsimd, i_planes["k"][:, 2:G, :])
-            nc.gpsimd.dma_start(out=bias_rows[0:12, :], in_=bias.rearrange("(j n) -> j n", n=N))
+            zero(nc.gpsimd, w_planes["k", I][:, 2:G, :])
+            nc.gpsimd.dma_start(out=bias_rows[0:16, :], in_=bias.rearrange("(j n) -> j n", n=NBIAS))
             make_identity(nc, ident[:])
             act(warm[:], warm[:], ACT.Sigmoid)
-            for g in range(G):
-                zero(nc.gpsimd, i_planes["r"][:, g, :])
-            for m in "kr":
+            for m, a in (("r", I), ("k", F), ("r", F)):
                 for g in range(G):
-                    zero(nc.gpsimd, fo_planes[m][:, g, :])
-            for i in range(2 * NB):
-                bias_spread(i, NB * (I, F)[i // NB] + i % NB)
+                    zero(nc.gpsimd, w_planes[m, a][:, g, :])
+            pool_dma(cu_sb[:].rearrange("p s d -> p (s d)"), c_upd)
+            pool_dma(c_sb[:].rearrange("p s d -> p (s d)"), c_state)
+
+            def load_w(m, a, p0, p1):
+                src = k_words if m == "k" else r_words
+                load_codes(w_codes[m, a][:, p0:p1, :], src, p0, p1, D * a, D)
+
+            def load_w_scales(m, a, rows=range(4)):
+                load_scales(w_planes[m, a], k_scales if m == "k" else r_scales, D * a, D, rows)
 
             nc.sync.dma_start(out=x_codes[:].bitcast(I32), in_=x_words.rearrange("g p n -> p g n").bitcast(I32))
-            load_scales(x_planes, x_scales, slice(0, G), slice(0, B), range(0, 2))
-            load_codes("k", I, 0, 1)
-            load_scales(x_planes, x_scales, slice(0, G), slice(0, B), range(2, 4))
-            load_i_scales("k")
-            load_codes("k", I, 1, 2)
-            load_codes("k", I, 2, 3)
+            load_scales(x_planes, x_scales, 0, B, range(0, 2))
+            load_w("k", I, 0, 1)
+            load_scales(x_planes, x_scales, 0, B, range(2, 4))
+            load_w_scales("k", I)
+            load_w("k", I, 1, 2)
+            load_w("k", I, 2, 4)
             nc.sync.dma_start(out=h_raw[:].bitcast(I32), in_=h_words.rearrange("g p n -> p g n").bitcast(I32))
-            load_scales(h_raw_planes, h_scales, slice(0, G), slice(0, S * B))
-            load_codes("k", I, 3, 4)
-            load_i_scales("r")
-            load_half(cu_sb, c_upd, 0)
-            load_codes("r", I, 0, 2, 0)
-            load_codes("r", I, 2, 4, 0)
-            load_half(cu_sb, c_upd, 1)
-            load_codes("r", I, 0, 2, 1)
-            load_codes("r", I, 2, 4, 1)
-            load_fo_scales("k")
-            load_fo_scales("r")
-            load_codes("k", F, 0, 2)
-            load_codes("k", F, 2, 4)
-            for half in range(2):
-                load_half(c_sb, c_state, half)
-                load_codes("r", F, 0, 2, half)
-                load_codes("r", F, 2, 4, half)
+            load_scales(h_raw_planes, h_scales, 0, S * B)
+            load_w("r", I, 0, 2)
+            load_w_scales("r", I)
+            load_w("r", I, 2, 4)
+            load_w_scales("k", F)
+            load_w("k", F, 0, 2)
+            load_w("k", F, 2, 4)
+            load_w_scales("r", F)
+            load_w("r", F, 0, 2)
+            load_w("r", F, 2, 4)
+
+            for j in range(3 * D // NBIAS):
+                bias_spread(j)
 
             for s in range(S):
                 nc.vector.tensor_copy(
@@ -205,111 +203,120 @@ def tile_rlstmcell_pb_kernel(
                     in_=h_raw_planes[:].rearrange("p g (b s) -> p g b s", s=S)[:, :, :, s],
                 )
 
-            def h_unit(a, b, xzb):
-                z = new_z()
-                accs = [new_acc() for s in range(S)]
-                for g in range(G):
-                    for s in range(S):
-                        h_pass(accs[s], s, a, g, N * b, N)
-                for s in range(S):
-                    z_add(z, s, accs[s], xzb)
-                return z
+            tasks = []
+            unit = 0
 
-            accs = [new_acc() for b in range(NB)]
-            for g in range(G):
-                for b in range(NB):
-                    x_pass(accs[b], I, b, g)
-            for j in range(NB):
-                bias_spread(j, NB * O + j)
-            xzbs = [x_drain(accs[b], I, b) for b in range(NB)]
-            inputs = []
-            h_tiles = []
-
-            def new_state(b, z):
-                nc.vector.tensor_tensor(out=cn[b][:], in0=z[:], in1=cn[b][:], op=ALU.add)
-                ht = work.tile([P, S, N], F32, name="ht", bufs=4)
-                act(ht[:], cn[b][:], ACT.Tanh)
-                h_tiles.append(ht)
-                nc.sync.dma_start(out=c_out_3d[:, :, blk(b)], in_=cn[b][:])
-
-            def x_gate(a, between=()):
-                out = []
-                for b in range(NB):
-                    acc = new_acc()
-                    for g in range(G):
-                        x_pass(acc, a, b, g)
-                    out.append(x_drain(acc, a, b))
-                    for step in between[b : b + 1]:
-                        step()
-                return out
-
-            def forget_product(engine, b, s, z):
-                engine.tensor_tensor(out=z[:, s, :], in0=z[:, s, :], in1=half_block(c_sb, b)[:, s, :], op=ALU.mult)
+            def run_tasks(most=99):
+                while tasks and tasks[0][0] <= unit and most > 0:
+                    tasks.pop(0)[1]()
+                    most -= 1
 
             def in_product(b, z):
-                nc.vector.tensor_tensor(out=cn[b][:], in0=z[:], in1=cn[b][:], op=ALU.mult)
+                mul(nc.vector, cn[:, :, blk(b)], z[:], cn[:, :, blk(b)])
 
-            for b in range(NB):
-                z = h_unit(I, b, xzbs[b])
-                act(cn[b][:], half_block(cu_sb, b), ACT.Tanh)
-                act(z[:], z[:], ACT.Sigmoid)
-                if inputs:
-                    in_product(*inputs.pop())
-                inputs.append((b, z))
+            def forget(engine, b, s, z):
+                mul(engine, z[:, s, :], z[:, s, :], c_sb[:, s, blk(b)])
 
-            load_codes("k", O, 0, 2)
-            load_codes("k", O, 2, 4)
-            for part in range(2):
-                for g in (0, 2):
-                    load_codes("r", O, g, g + 2, part)
+            def new_state(b, z):
+                at = cn[:, :, blk(b)]
+                nc.vector.tensor_tensor(out=at, in0=z[:], in1=at, op=ALU.add)
+                act(ht[:, :, blk(b)], at, ACT.Tanh)
+                if b == NB - 1:
+                    pool_dma(c_out, cn[:].rearrange("p s d -> p (s d)"))
 
-            xzbs = x_gate(F)
-            zs = []
-            for b in range(NB):
-                z = h_unit(F, b, xzbs[b])
-                zs.append(z)
-                act(z[:], z[:], ACT.Sigmoid)
-                forget_product(nc.gpsimd, b, 0, z)
-                if b % 2 == 0:
-                    forget_product(nc.gpsimd, b, 1, z)
-                if b == 0:
-                    in_product(*inputs.pop())
-                elif b == 2:
-                    forget_product(nc.vector, 1, 1, zs[1])
-                    new_state(0, zs[0])
-                elif b == 3:
-                    new_state(1, zs[1])
+            def out_product(b, z, s0, s1, off, n):
+                at = slice(N * b + off, N * b + off + n)
+                engine = nc.gpsimd if b == 0 else nc.vector
+                mul(engine, ht[:, s0:s1, at], z[:, s0:s1, off : off + n], ht[:, s0:s1, at])
 
-            between = (
-                lambda: forget_product(nc.vector, 3, 1, zs[3]),
-                lambda: new_state(2, zs[2]),
-                lambda: None,
-                lambda: new_state(3, zs[3]),
-            )
-            xzbs = x_gate(O, between)
-            pending = []
+            def store_h(s0, s1, c0, n):
+                cols = slice(c0, c0 + n)
+                nc.sync.dma_start(out=h_out[:, s0:s1, cols], in_=ht[:, s0:s1, cols])
 
-            def out_product(b, ht, z, s0, s1, off, n):
-                at = slice(off, off + n)
-                nc.vector.tensor_tensor(out=ht[:, s0:s1, at], in0=z[:, s0:s1, at], in1=ht[:, s0:s1, at], op=ALU.mult)
-                nc.sync.dma_start(out=h_out_3d[:, s0:s1, N * b + off : N * b + off + n], in_=ht[:, s0:s1, at])
-
-            for b in range(NB):
-                ht = h_tiles[b]
-                if b < NB - 1:
-                    z = h_unit(O, b, xzbs[b])
-                    act(z[:], z[:], ACT.Sigmoid)
-                    if pending:
-                        out_product(*pending.pop())
-                    pending.append((b, ht, z, 0, S, 0, N))
-                else:
-                    z = new_z()
-                    for s, off, n in ((0, 0, N), (1, 0, N // 2), (1, N // 2, N // 2)):
-                        acc = new_acc()
+            def x_gate(a):
+                out = {}
+                accs = {b: new_acc() for b in range(NB)}
+                if a == I:
+                    for g in range(G):
+                        for b in range(NB):
+                            x_pass(accs[b], a, b, g)
+                for b in range(NB):
+                    if a != I:
                         for g in range(G):
+                            x_pass(accs[b], a, b, g)
+                    if a == O and b == 0:
+                        run_tasks()
+                    out[b] = x_drain(accs[b], a, b)
+                return out
+
+            for a in (I, F):
+                xzbs = x_gate(a)
+                for half in range(2):
+                    blocks = (2 * half, 2 * half + 1)
+                    accs = {(b, s): new_acc() for b in blocks for s in range(S)}
+                    for b in blocks:
+                        for s in range(S):
+                            for g in (0, 1):
+                                h_pass(accs[b, s], s, a, g, N * b, N)
+                    for b in blocks:
+                        for s in range(S):
+                            for g in (2, 3):
+                                h_pass(accs[b, s], s, a, g, N * b, N)
+                    for b in blocks:
+                        z = new_z()
+                        for s in range(S):
+                            z_add(z, s, accs[b, s], xzbs[b])
+                        act(z[:], z[:], ACT.Sigmoid)
+                        run_tasks()
+                        unit += 1
+                        if a == I:
+                            act(cn[:, :, blk(b)], cu_sb[:, :, blk(b)], ACT.Tanh)
+                            tasks.append((unit, partial(in_product, b, z)))
+                        else:
+                            forget(nc.gpsimd, b, 0, z)
+                            if b % 2 == 0:
+                                forget(nc.gpsimd, b, 1, z)
+                            else:
+                                tasks.append((unit, partial(forget, nc.vector, b, 1, z)))
+                            tasks.append((unit + 1, partial(new_state, b, z)))
+                if a == I:
+                    load_w_scales("k", O)
+                    load_w("k", O, 0, 2)
+                    load_w("k", O, 2, 4)
+                    load_w_scales("r", O)
+                    for j in range(2):
+                        for g in (0, 2):
+                            load_codes(r_o_codes[j][:, g : g + 2, :], r_words, g, g + 2, 2 * D + 2 * N * j, 2 * N)
+
+            unit += 2
+            xzbs = x_gate(O)
+            run_tasks()
+            pieces = [(b, s, 0, N) for b, s in ((0, 0), (0, 1), (1, 0), (1, 1), (2, 0), (3, 0), (2, 1))]
+            pieces += [(3, 1, 0, N // 2), (3, 1, N // 2, N // 2)]
+            stores = {
+                (1, 1, 0): (0, S, 0, 2 * N),
+                (3, 0, 0): (0, 1, 2 * N, 2 * N),
+                (2, 1, 0): (1, 2, 2 * N, N),
+                (3, 1, N // 2): (1, 2, 3 * N, N),
+            }
+            pending = None
+
+            def finish(b, s, off, n, z):
+                out_product(b, z, s, s + 1, off, n)
+                if (b, s, off) in stores:
+                    store_h(*stores[b, s, off])
+
+            for group in (pieces[0:4], pieces[4:]):
+                accs = [new_acc() for piece in group]
+                for passes in ((0, 1), (2, 3)):
+                    for acc, (b, s, off, n) in zip(accs, group):
+                        for g in passes:
                             h_pass(acc, s, O, g, N * b + off, n)
-                        z_add(z, s, acc, xzbs[b], off, n)
-                        act(z[:, s, off : off + n], z[:, s, off : off + n], ACT.Sigmoid)
-                        out_product(*pending.pop())
-                        pending.append((b, ht, z, s, s + 1, off, n))
-            out_product(*pending.pop())
+                for acc, (b, s, off, n) in zip(accs, group):
+                    z = new_z()
+                    z_add(z, s, acc, xzbs[b], off, n)
+                    act(z[:, s, off : off + n], z[:, s, off : off + n], ACT.Sigmoid)
+                    if pending is not None:
+                        finish(*pending)
+                    pending = (b, s, off, n, z)
+            finish(*pending)

@@ -21,8 +21,6 @@ I, F, O = range(3)
 
 NBIAS = 384
 
-ROW_PARTS = (slice(0, 4), slice(4, 112), slice(112, P))
-
 FLOPS = 2 * (B + B * S) * D * 3 * D
 
 
@@ -88,10 +86,6 @@ def tile_rlstmcell_pb_kernel(
                 in_=src[p0:p1, :, 2 * c0 : 2 * (c0 + n)].rearrange("g p n -> p g n").bitcast(I32),
             )
 
-        def pool_dma(out, in_):
-            for rows in ROW_PARTS:
-                nc.gpsimd.dma_start(out=out[rows], in_=in_[rows])
-
         def zero(engine, ap):
             engine.memset(ap.bitcast(I32), 0)
 
@@ -99,22 +93,22 @@ def tile_rlstmcell_pb_kernel(
             acc = psum.tile([P, N], F32, name="acc")
             return acc
 
-        def mm(acc_ap, lhs, lhs_scale, rhs, g):
+        def mm(acc_ap, lhs, lhs_scale, rhs, start, stop):
             nc.tensor.matmul_mx(
                 out=acc_ap,
                 lhsT=lhs.bitcast(FP4X4),
                 lhsT_scale=lhs_scale,
                 rhs=rhs[0].bitcast(FP4X4),
                 rhs_scale=rhs[1],
-                start=(g == 0),
-                stop=(g == G - 1),
+                start=start,
+                stop=stop,
             )
 
-        def x_pass(acc, a, b, g):
-            mm(acc[:], x_codes[:, g, :], x_planes[:, g, :], operand("k", a, g, N * b, N), g)
+        def x_pass(acc, a, b, g, alone=True):
+            mm(acc[:], x_codes[:, g, :], x_planes[:, g, :], operand("k", a, g, N * b, N), g == 0, alone and g == G - 1)
 
-        def h_pass(acc, s, a, g, c0, n):
-            mm(acc[:, 0:n], h_codes[:, s, g, :], h_planes[:, s, g, :], operand("r", a, g, c0, n), g)
+        def h_pass(acc, s, a, g, c0, n, alone=True):
+            mm(acc[:, 0:n], h_codes[:, s, g, :], h_planes[:, s, g, :], operand("r", a, g, c0, n), alone and g == 0, g == G - 1)
 
         def bias_spread(j):
             acc = new_acc()
@@ -160,8 +154,6 @@ def tile_rlstmcell_pb_kernel(
             for m, a in (("r", I), ("k", F), ("r", F)):
                 for g in range(G):
                     zero(nc.gpsimd, w_planes[m, a][:, g, :])
-            pool_dma(cu_sb[:].rearrange("p s d -> p (s d)"), c_upd)
-            pool_dma(c_sb[:].rearrange("p s d -> p (s d)"), c_state)
 
             def load_w(m, a, p0, p1):
                 src = k_words if m == "k" else r_words
@@ -182,12 +174,14 @@ def tile_rlstmcell_pb_kernel(
             load_w("r", I, 0, 2)
             load_w_scales("r", I)
             load_w("r", I, 2, 4)
-            load_w_scales("k", F)
+            nc.sync.dma_start(out=cu_sb[:].rearrange("p s d -> p (s d)"), in_=c_upd)
             load_w("k", F, 0, 2)
+            load_w_scales("k", F)
             load_w("k", F, 2, 4)
-            load_w_scales("r", F)
             load_w("r", F, 0, 2)
+            load_w_scales("r", F)
             load_w("r", F, 2, 4)
+            nc.sync.dma_start(out=c_sb[:].rearrange("p s d -> p (s d)"), in_=c_state)
 
             for j in range(3 * D // NBIAS):
                 bias_spread(j)
@@ -222,12 +216,11 @@ def tile_rlstmcell_pb_kernel(
                 nc.vector.tensor_tensor(out=at, in0=z[:], in1=at, op=ALU.add)
                 act(ht[:, :, blk(b)], at, ACT.Tanh)
                 if b == NB - 1:
-                    pool_dma(c_out, cn[:].rearrange("p s d -> p (s d)"))
+                    nc.sync.dma_start(out=c_out, in_=cn[:].rearrange("p s d -> p (s d)"))
 
             def out_product(b, z, s0, s1, off, n):
                 at = slice(N * b + off, N * b + off + n)
-                engine = nc.gpsimd if b == 0 else nc.vector
-                mul(engine, ht[:, s0:s1, at], z[:, s0:s1, off : off + n], ht[:, s0:s1, at])
+                mul(nc.vector, ht[:, s0:s1, at], z[:, s0:s1, off : off + n], ht[:, s0:s1, at])
 
             def store_h(s0, s1, c0, n):
                 cols = slice(c0, c0 + n)
@@ -244,11 +237,10 @@ def tile_rlstmcell_pb_kernel(
                     if a != I:
                         for g in range(G):
                             x_pass(accs[b], a, b, g)
-                    if a == O and b == 0:
-                        run_tasks()
                     out[b] = x_drain(accs[b], a, b)
                 return out
 
+            first_add = 7
             for a in (I, F):
                 xzbs = x_gate(a)
                 for half in range(2):
@@ -273,24 +265,38 @@ def tile_rlstmcell_pb_kernel(
                             act(cn[:, :, blk(b)], cu_sb[:, :, blk(b)], ACT.Tanh)
                             tasks.append((unit, partial(in_product, b, z)))
                         else:
-                            forget(nc.gpsimd, b, 0, z)
-                            if b % 2 == 0:
-                                forget(nc.gpsimd, b, 1, z)
-                            else:
-                                tasks.append((unit, partial(forget, nc.vector, b, 1, z)))
-                            tasks.append((unit + 1, partial(new_state, b, z)))
+                            for s in range(S):
+                                if b < 2:
+                                    forget(nc.gpsimd, b, s, z)
+                                else:
+                                    tasks.append((unit, partial(forget, nc.vector, b, s, z)))
+                            tasks.append((max(unit + 1, first_add), partial(new_state, b, z)))
                 if a == I:
-                    load_w_scales("k", O)
                     load_w("k", O, 0, 2)
+                    load_w_scales("k", O)
                     load_w("k", O, 2, 4)
-                    load_w_scales("r", O)
                     for j in range(2):
                         for g in (0, 2):
                             load_codes(r_o_codes[j][:, g : g + 2, :], r_words, g, g + 2, 2 * D + 2 * N * j, 2 * N)
+                            if j == 0 and g == 0:
+                                load_w_scales("r", O)
+                    unit += 1
+                    run_tasks()
 
             unit += 2
-            xzbs = x_gate(O)
+            accs = [new_acc() for i in range(4)]
+            for g in range(G):
+                for i in range(4):
+                    x_pass(accs[i], O, i // 2, g, alone=False)
             run_tasks()
+            xzbs = {}
+            for b in (2, 3):
+                acc = new_acc()
+                for g in range(G):
+                    x_pass(acc, O, b, g)
+                xzbs[b] = x_drain(acc, O, b)
+            for b in (0, 1):
+                xzbs[b] = bias_sb[:, D * O + N * b : D * O + N * (b + 1)]
             pieces = [(b, s, 0, N) for b, s in ((0, 0), (0, 1), (1, 0), (1, 1), (2, 0), (3, 0), (2, 1))]
             pieces += [(3, 1, 0, N // 2), (3, 1, N // 2, N // 2)]
             stores = {
@@ -306,12 +312,15 @@ def tile_rlstmcell_pb_kernel(
                 if (b, s, off) in stores:
                     store_h(*stores[b, s, off])
 
-            for group in (pieces[0:4], pieces[4:]):
-                accs = [new_acc() for piece in group]
+            first_group = pieces[0:4]
+            for group in (first_group, pieces[4:]):
+                alone = group is not first_group
+                if alone:
+                    accs = [new_acc() for piece in group]
                 for passes in ((0, 1), (2, 3)):
                     for acc, (b, s, off, n) in zip(accs, group):
                         for g in passes:
-                            h_pass(acc, s, O, g, N * b + off, n)
+                            h_pass(acc, s, O, g, N * b + off, n, alone)
                 for acc, (b, s, off, n) in zip(accs, group):
                     z = new_z()
                     z_add(z, s, acc, xzbs[b], off, n)

from functools import partial

import concourse.mybir as mybir
from concourse.masks import make_identity

F32 = mybir.dt.float32
BF16 = mybir.dt.bfloat16
I32 = mybir.dt.int32
U8 = mybir.dt.uint8
FP4X4 = mybir.dt.float4_e2m1fn_x4
ACT = mybir.ActivationFunctionType
ALU = mybir.AluOpType

P = 128
B, S, D = 128, 2, 2048
G = D // 512
N = 512
NB = D // N

I, F, O = range(3)

NBIAS = 384

FLOPS = 2 * (B + B * S) * D * 3 * D


def tile_rlstmcell_pb_kernel(
    tc, x_words, x_scales, h_words, h_scales, c_state, c_upd, k_words, k_scales, r_words, r_scales, bias, h_out, c_out
):
    nc = tc.nc
    c_upd = c_upd.rearrange("b s d -> b (s d)")
    h_out = h_out.rearrange("b (s d) -> b s d", s=S)

    with (
        tc.tile_pool(name="keep", bufs=1) as keep,
        tc.tile_pool(name="work", bufs=1) as work,
        tc.psum_pool(name="psum", bufs=8) as psum,
    ):
        def u8_tile(name, shape):
            return keep.tile(shape, U8, name=name, align_bytes=64)

        x_codes = u8_tile("x_codes", [P, G, 2 * B])
        x_planes = u8_tile("x_planes", [P, G, B])
        h_raw = u8_tile("h_raw", [P, G, 2 * S * B])
        h_raw_planes = u8_tile("h_raw_planes", [P, G, S * B])
        h_codes = u8_tile("h_codes", [P, S, G, 2 * B])
        h_planes = u8_tile("h_planes", [P, S, G, B])
        w_codes = {(m, a): u8_tile(f"{m}_codes_{a}", [P, G, 2 * D]) for m in "kr" for a in (I, F)}
        w_planes = {(m, a): u8_tile(f"{m}_planes_{a}", [P, G, D]) for m in "kr" for a in (I, F)}
        for m in "kr":
            w_planes[m, O] = w_planes[m, I]
        w_codes["k", O] = w_codes["k", I]
        r_flat = w_codes["r", I][:].rearrange("p g n -> p (g n)")
        r_o_codes = [r_flat[:, 4 * D * j : 4 * D * (j + 1)].rearrange("p (g n) -> p g n", g=G) for j in range(2)]

        def operand(m, a, g, c0, n):
            if (m, a) == ("r", O):
                at = 2 * (c0 % (2 * N))
                codes = r_o_codes[c0 // (2 * N)][:, g, at : at + 2 * n]
            else:
                codes = w_codes[m, a][:, g, 2 * c0 : 2 * (c0 + n)]
            return codes, w_planes[m, a][:, g, c0 : c0 + n]

        ident = keep.tile([P, P], BF16, name="ident")
        bias_rows = keep.tile([P, NBIAS], BF16, name="bias_rows")
        bias_sb = keep.tile([P, 3 * D], BF16, name="bias_sb")
        cu_sb = keep.tile([P, S, D], BF16, name="cu_sb")
        c_sb = keep.tile([P, S, D], BF16, name="c_sb")
        cn = keep.tile([P, S, D], F32, name="cn")
        ht = keep.tile([P, S, D], F32, name="ht")
        warm = keep.tile([P, 1], F32, name="warm")

        def blk(b):
            return slice(N * b, N * (b + 1))

        def load_scales(planes, src, c0, n, rows=range(4)):
            for r in rows:
                nc.sync.dma_start(
                    out=planes[r:P:32, :, :].bitcast(I32),
                    in_=src[:, r:16:4, c0 : c0 + n].rearrange("g q n -> q g n").bitcast(I32),
                )

        def load_codes(codes, src, p0, p1, c0, n):
            nc.sync.dma_start(
                out=codes.bitcast(I32),
                in_=src[p0:p1, :, 2 * c0 : 2 * (c0 + n)].rearrange("g p n -> p g n").bitcast(I32),
            )

        def zero(engine, ap):
            engine.memset(ap.bitcast(I32), 0)

        def new_acc():
            acc = psum.tile([P, N], F32, name="acc")
            return acc

        def mm(acc_ap, lhs, lhs_scale, rhs, start, stop):
            nc.tensor.matmul_mx(
                out=acc_ap,
                lhsT=lhs.bitcast(FP4X4),
                lhsT_scale=lhs_scale,
                rhs=rhs[0].bitcast(FP4X4),
                rhs_scale=rhs[1],
                start=start,
                stop=stop,
            )

        def x_pass(acc, a, b, g, alone=True):
            mm(acc[:], x_codes[:, g, :], x_planes[:, g, :], operand("k", a, g, N * b, N), g == 0, alone and g == G - 1)

        def h_pass(acc, s, a, g, c0, n, alone=True):
            mm(acc[:, 0:n], h_codes[:, s, g, :], h_planes[:, s, g, :], operand("r", a, g, c0, n), alone and g == 0, g == G - 1)

        def bias_spread(j):
            acc = new_acc()
            nc.tensor.matmul(
                acc[:, 0:NBIAS], lhsT=ident[:, j : j + 1].to_broadcast([P, P]), rhs=bias_rows[:], start=True, stop=True
            )
            out = bias_sb[:, NBIAS * j : NBIAS * (j + 1)]
            if j % 2 == 0:
                nc.scalar.copy(out=out, in_=acc[:, 0:NBIAS])
            else:
                nc.vector.tensor_copy(out=out, in_=acc[:, 0:NBIAS])

        def x_drain(acc, a, b):
            xzb = work.tile([P, N], F32, name="xzb", bufs=8)
            c0 = D * a + N * b
            nc.vector.tensor_tensor(out=xzb[:], in0=acc[:], in1=bias_sb[:, c0 : c0 + N], op=ALU.add)
            return xzb

        def new_z():
            z = work.tile([P, S, N], F32, name="z", bufs=6)
            return z

        def z_add(z, s, acc, xzb, off=0, n=N):
            at = slice(off, off + n)
            nc.vector.tensor_tensor(out=z[:, s, at], in0=acc[:, 0:n], in1=xzb[:, at], op=ALU.add)

        def act(out, in_, func):
            nc.scalar.activation(out=out, in_=in_, func=func)

        def mul(engine, out, in0, in1):
            engine.tensor_tensor(out=out, in0=in0, in1=in1, op=ALU.mult)

        with tc.manual_schedule():
            nc.vector.memset(warm[:], 0.0)
            zero(nc.vector, x_planes[:])
            nc.vector.memset(bias_rows[:], 0.0)
            zero(nc.vector, w_planes["k", I][:, 0:2, :])
            zero(nc.vector, h_raw_planes[:])
            zero(nc.gpsimd, w_planes["k", I][:, 2:G, :])
            nc.gpsimd.dma_start(out=bias_rows[0:16, :], in_=bias.rearrange("(j n) -> j n", n=NBIAS))
            make_identity(nc, ident[:])
            act(warm[:], warm[:], ACT.Sigmoid)
            for m, a in (("r", I), ("k", F), ("r", F)):
                for g in range(G):
                    zero(nc.gpsimd, w_planes[m, a][:, g, :])

            def load_w(m, a, p0, p1):
                src = k_words if m == "k" else r_words
                load_codes(w_codes[m, a][:, p0:p1, :], src, p0, p1, D * a, D)

            def load_w_scales(m, a, rows=range(4)):
                load_scales(w_planes[m, a], k_scales if m == "k" else r_scales, D * a, D, rows)

            nc.sync.dma_start(out=x_codes[:].bitcast(I32), in_=x_words.rearrange("g p n -> p g n").bitcast(I32))
            load_scales(x_planes, x_scales, 0, B, range(0, 2))
            load_w("k", I, 0, 1)
            load_scales(x_planes, x_scales, 0, B, range(2, 4))
            load_w_scales("k", I)
            load_w("k", I, 1, 2)
            load_w("k", I, 2, 4)
            nc.sync.dma_start(out=h_raw[:].bitcast(I32), in_=h_words.rearrange("g p n -> p g n").bitcast(I32))
            load_scales(h_raw_planes, h_scales, 0, S * B)
            load_w("r", I, 0, 2)
            load_w_scales("r", I)
            load_w("r", I, 2, 4)
            nc.sync.dma_start(out=cu_sb[:].rearrange("p s d -> p (s d)"), in_=c_upd)
            load_w("k", F, 0, 2)
            load_w_scales("k", F)
            load_w("k", F, 2, 4)
            load_w("r", F, 0, 2)
            load_w_scales("r", F)
            load_w("r", F, 2, 4)
            nc.sync.dma_start(out=c_sb[:].rearrange("p s d -> p (s d)"), in_=c_state)

            for j in range(3 * D // NBIAS):
                bias_spread(j)

            for s in range(S):
                nc.vector.tensor_copy(
                    out=h_codes[:, s, :, :].rearrange("p g (b t) -> p g b t", t=2),
                    in_=h_raw[:].rearrange("p g (b s t) -> p g b s t", s=S, t=2)[:, :, :, s, :],
                )
            for s in range(S):
                nc.vector.tensor_copy(
                    out=h_planes[:, s, :, :],
                    in_=h_raw_planes[:].rearrange("p g (b s) -> p g b s", s=S)[:, :, :, s],
                )

            tasks = []
            unit = 0

            def run_tasks(most=99):
                while tasks and tasks[0][0] <= unit and most > 0:
                    tasks.pop(0)[1]()
                    most -= 1

            def in_product(b, z):
                mul(nc.vector, cn[:, :, blk(b)], z[:], cn[:, :, blk(b)])

            def forget(engine, b, s, z):
                mul(engine, z[:, s, :], z[:, s, :], c_sb[:, s, blk(b)])

            def new_state(b, z):
                at = cn[:, :, blk(b)]
                nc.vector.tensor_tensor(out=at, in0=z[:], in1=at, op=ALU.add)
                act(ht[:, :, blk(b)], at, ACT.Tanh)
                if b == NB - 1:
                    nc.sync.dma_start(out=c_out, in_=cn[:].rearrange("p s d -> p (s d)"))

            def out_product(b, z, s0, s1, off, n):
                at = slice(N * b + off, N * b + off + n)
                mul(nc.vector, ht[:, s0:s1, at], z[:, s0:s1, off : off + n], ht[:, s0:s1, at])

            def store_h(s0, s1, c0, n):
                cols = slice(c0, c0 + n)
                nc.sync.dma_start(out=h_out[:, s0:s1, cols], in_=ht[:, s0:s1, cols])

            def x_gate(a):
                out = {}
                accs = {b: new_acc() for b in range(NB)}
                if a == I:
                    for g in range(G):
                        for b in range(NB):
                            x_pass(accs[b], a, b, g)
                for b in range(NB):
                    if a != I:
                        for g in range(G):
                            x_pass(accs[b], a, b, g)
                    out[b] = x_drain(accs[b], a, b)
                return out

            first_add = 7
            for a in (I, F):
                xzbs = x_gate(a)
                for half in range(2):
                    blocks = (2 * half, 2 * half + 1)
                    accs = {(b, s): new_acc() for b in blocks for s in range(S)}
                    for b in blocks:
                        for s in range(S):
                            for g in (0, 1):
                                h_pass(accs[b, s], s, a, g, N * b, N)
                    for b in blocks:
                        for s in range(S):
                            for g in (2, 3):
                                h_pass(accs[b, s], s, a, g, N * b, N)
                    for b in blocks:
                        z = new_z()
                        for s in range(S):
                            z_add(z, s, accs[b, s], xzbs[b])
                        act(z[:], z[:], ACT.Sigmoid)
                        run_tasks()
                        unit += 1
                        if a == I:
                            act(cn[:, :, blk(b)], cu_sb[:, :, blk(b)], ACT.Tanh)
                            tasks.append((unit, partial(in_product, b, z)))
                        else:
                            for s in range(S):
                                if b < 2:
                                    forget(nc.gpsimd, b, s, z)
                                else:
                                    tasks.append((unit, partial(forget, nc.vector, b, s, z)))
                            tasks.append((max(unit + 1, first_add), partial(new_state, b, z)))
                if a == I:
                    load_w("k", O, 0, 2)
                    load_w_scales("k", O)
                    load_w("k", O, 2, 4)
                    for j in range(2):
                        for g in (0, 2):
                            load_codes(r_o_codes[j][:, g : g + 2, :], r_words, g, g + 2, 2 * D + 2 * N * j, 2 * N)
                            if j == 0 and g == 0:
                                load_w_scales("r", O)
                    unit += 1
                    run_tasks()

            unit += 2
            accs = [new_acc() for i in range(4)]
            for g in range(G):
                for i in range(4):
                    x_pass(accs[i], O, i // 2, g, alone=False)
            run_tasks()
            xzbs = {}
            for b in (2, 3):
                acc = new_acc()
                for g in range(G):
                    x_pass(acc, O, b, g)
                xzbs[b] = x_drain(acc, O, b)
            for b in (0, 1):
                xzbs[b] = bias_sb[:, D * O + N * b : D * O + N * (b + 1)]
            pieces = [(b, s, 0, N) for b, s in ((0, 0), (0, 1), (1, 0), (1, 1), (2, 0), (3, 0), (2, 1))]
            pieces += [(3, 1, 0, N // 2), (3, 1, N // 2, N // 2)]
            stores = {
                (1, 1, 0): (0, S, 0, 2 * N),
                (3, 0, 0): (0, 1, 2 * N, 2 * N),
                (2, 1, 0): (1, 2, 2 * N, N),
                (3, 1, N // 2): (1, 2, 3 * N, N),
            }
            pending = None

            def finish(b, s, off, n, z):
                out_product(b, z, s, s + 1, off, n)
                if (b, s, off) in stores:
                    store_h(*stores[b, s, off])

            first_group = pieces[0:4]
            for group in (first_group, pieces[4:]):
                alone = group is not first_group
                if alone:
                    accs = [new_acc() for piece in group]
                for passes in ((0, 1), (2, 3)):
                    for acc, (b, s, off, n) in zip(accs, group):
                        for g in passes:
                            h_pass(acc, s, O, g, N * b + off, n, alone)
                for acc, (b, s, off, n) in zip(accs, group):
                    z = new_z()
                    z_add(z, s, acc, xzbs[b], off, n)
                    act(z[:, s, off : off + n], z[:, s, off : off + n], ACT.Sigmoid)
                    if pending is not None:
                        finish(*pending)
                    pending = (b, s, off, n, z)
            finish(*pending)
